import numpy as np
import ml_dtypes


def mxq(x, axis, fmt="e4m3"):
    dtype, down = {"e4m3": (ml_dtypes.float8_e4m3fn, 7), "e5m2": (ml_dtypes.float8_e5m2, 14)}[fmt]
    v = np.moveaxis(np.asarray(x, np.float32).astype(ml_dtypes.bfloat16).astype(np.float64), axis, -1)
    blocks = v.reshape(v.shape[:-1] + (-1, 32))
    amax = np.abs(blocks).max(-1, keepdims=True)
    byte = np.maximum(np.where(amax > 0, np.frexp(amax)[1] - 1 + 127, 0) - down, 1)
    scale = np.exp2(byte - 127.0)
    codes = (blocks / scale).astype(np.float32).astype(dtype).astype(np.float64)
    return np.moveaxis((codes * scale).reshape(v.shape), -1, axis)


WIDE = False


def mx_kscale(k):
    if not WIDE:
        return np.ones(k)
    levels = np.array([10, -10, 5, -5, 0])
    if k % 512:
        return np.exp2(np.random.permutation(np.resize(levels, k // 32))).repeat(32)
    a = np.empty((k // 512, 16))
    for p in range(k // 512):
        a[p, :8] = np.random.permutation(np.resize(levels, 8))
        for g in range(8):
            far = levels[np.abs(levels - a[p, g]) >= 10]
            a[p, g + 8] = far[np.random.randint(len(far))]
    return np.exp2(a.ravel()).repeat(32)


BF16 = ml_dtypes.bfloat16


def bf(x):
    return np.asarray(x, np.float32).astype(BF16)


def f64(x):
    return np.asarray(x).astype(np.float64)


B, N, D_IN, H, D_HEAD, D_EXPAND = 4, 1536, 2048, 1, 128, 2048
D_V = D_IN * H
EPS = 1e-5


def feature_norm(x, gamma, beta):
    mean = x.mean(axis=1, keepdims=True)
    var = x.var(axis=1, keepdims=True)
    return gamma * (x - mean) / np.sqrt(var + EPS) + beta


def setup_inputs():
    t = mx_kscale(D_V)
    s = mx_kscale(D_IN)
    return {"attn_out": bf(5.0 * np.random.standard_normal((B, N, D_V)) * t),
            "x": bf(1.5 * np.random.standard_normal((B, N, D_IN))),
            "W_merge": bf(np.random.standard_normal((D_V, D_IN)) * 0.2 / np.sqrt(D_V) / t[:, None]),
            "b_merge": bf(0.3 * np.random.standard_normal(D_IN)),
            "gamma2": bf((1.0 + 0.1 * np.random.standard_normal((1, 1, D_IN))) * s),
            "beta2": bf(0.2 * np.random.standard_normal((1, 1, D_IN)) * s),
            "W1": bf(np.random.standard_normal((D_IN, D_EXPAND)) / np.sqrt(D_IN) / s[:, None]),
            "b1": bf(0.2 * np.random.standard_normal(D_EXPAND))}


def reference(attn_out, x, W_merge, b_merge, gamma2, beta2, W1, b1):
    x2 = f64(x) + (mxq(f64(attn_out), 2, "e4m3") @ mxq(f64(W_merge), 0, "e4m3")) + f64(b_merge)
    xn = feature_norm(x2, f64(gamma2), f64(beta2))
    ffh = (mxq(xn, 2, "e4m3") @ mxq(f64(W1), 0, "e4m3")) + f64(b1)
    return x2, ffh

@@ -1,0 +1,539 @@
+from contextlib import ExitStack
+
+import concourse.mybir as mybir
+from concourse.masks import make_identity
+
+FLOPS = 2 * 2 * 4 * 1536 * 2048 * 2048
+
+F32 = mybir.dt.float32
+BF16 = mybir.dt.bfloat16
+U32 = mybir.dt.uint32
+U8 = mybir.dt.uint8
+FP8X4 = mybir.dt.float8_e4m3fn_x4
+ALU = mybir.AluOpType
+ACT = mybir.ActivationFunctionType
+
+P = 128
+NTOK = 1536
+EPS = 1e-5
+
+N_BUF = 12
+RESERVE = 4
+XT_BUFS = 2
+X2T_BUFS = 5
+XN_BUFS = 48
+RUN = 4
+HORIZON = 14
+D_SQ = 2
+D_NRM = 3
+D_ILV = 3
+D_QX = 1
+D_QA = 1
+D_ST = 1
+W_EVERY = 4
+W_START = 30
+D_WQ = 5
+B1_AT = 150
+VEC = 0
+SCA = 1
+GPS = 2
+
+
+def wm_engine(a, c):
+    if a == 0:
+        return (VEC, SCA, GPS, VEC)[c]
+    return GPS
+
+
+def nrm_engine(b, t):
+    if b == 0:
+        return (SCA, VEC, SCA, VEC)[t]
+    return VEC
+
+
+def tb_engine(b, i):
+    if b == 0:
+        return (SCA, SCA, VEC)[i % 3]
+    return SCA
+
+
+def ta_engine(b, i, h):
+    if b == 0:
+        return (VEC, SCA)[h]
+    return SCA
+
+
+def tile_attentionblock_pc_l_kernel(
+    tc, attn_out, x, W_merge, b_merge, gamma2, beta2, W1, b1, out_0, out_1
+):
+    nc = tc.nc
+    with ExitStack() as ctx:
+        keep = ctx.enter_context(tc.tile_pool(name="keep", bufs=1))
+        work = ctx.enter_context(tc.tile_pool(name="work", bufs=2))
+        small = ctx.enter_context(tc.tile_pool(name="small", bufs=8))
+        psum = ctx.enter_context(tc.psum_pool(name="psum", bufs=4))
+        ctx.enter_context(tc.manual_schedule())
+
+        ident = keep.tile([P, P], F32, name="ident")
+        make_identity(nc, ident[:])
+        neg_half = keep.tile([P, 1], F32, name="neg_half")
+        nc.vector.memset(neg_half[:], -0.5)
+
+        wm_codes = keep.tile([P, 4, 2048], U32, name="wm_codes", align_bytes=64)
+        wm_planes = keep.tile([P, 2048], U8, name="wm_planes", align_bytes=64)
+        w1_codes = keep.tile([P, 4, 2048], U32, name="w1_codes", align_bytes=64)
+        w1_planes = keep.tile([P, 2048], U8, name="w1_planes", align_bytes=64)
+        b1_rows = keep.tile([P, 2048], BF16, name="b1_rows")
+
+        bm_bf = keep.tile([P, 4, 4], BF16, name="bm_bf")
+        ga_bf = keep.tile([P, 4, 4], BF16, name="ga_bf")
+        be_bf = keep.tile([P, 4, 4], BF16, name="be_bf")
+        bm = keep.tile([P, 16], F32, name="bm")
+        ga = keep.tile([P, 16], F32, name="ga")
+        be = keep.tile([P, 16], F32, name="be")
+
+        st = {}
+        todo = {}
+        now = [0]
+        live = [0]
+        free_xn = [XN_BUFS]
+        ilv_wait = []
+
+        def later(d, item):
+            when = now[0] + d
+            if when not in todo:
+                todo[when] = []
+            todo[when].append(item)
+
+        def buf_bf16():
+            live[0] = live[0] + 1
+            assert live[0] <= N_BUF
+            buf = work.tile([P, 2048], BF16, name="buf", tag="buf", bufs=N_BUF, align_bytes=64)
+            return buf
+
+        def buf_f32():
+            live[0] = live[0] + 1
+            assert live[0] <= N_BUF
+            buf = work.tile([P, 1024], F32, name="buf", tag="buf", bufs=N_BUF, align_bytes=64)
+            return buf
+
+        def drop():
+            live[0] = live[0] - 1
+
+        def copy_on(which, out, in_):
+            if which == VEC:
+                nc.vector.tensor_copy(out=out, in_=in_)
+            elif which == SCA:
+                nc.scalar.copy(out=out, in_=in_)
+            else:
+                nc.gpsimd.tensor_scalar(out=out, in0=in_, scalar1=1.0, scalar2=0.0, op0=ALU.mult, op1=ALU.add)
+
+        def emit_load(key):
+            raw = buf_bf16()
+            if key[0] == "W":
+                src = W_merge if key[1] == "WM" else W1
+                a, c = key[2], key[3]
+                nc.sync.dma_start(
+                    out=raw[:].rearrange("p (j n) -> p j n", j=4),
+                    in_=src[512 * c : 512 * (c + 1), 512 * a : 512 * (a + 1)].rearrange("(p j) n -> p j n", j=4),
+                )
+            elif key[0] == "A":
+                b, i = key[1], key[2]
+                nc.sync.dma_start(out=raw[:], in_=attn_out[b, P * i : P * (i + 1), :])
+            else:
+                b, g, j = key[1], key[2], key[3]
+                nc.sync.dma_start(
+                    out=raw[:].rearrange("p (i c) -> p i c", i=4),
+                    in_=x[b, 512 * j : 512 * (j + 1), 512 * g : 512 * (g + 1)].rearrange("(i p) c -> p i c", p=P),
+                )
+            st[key] = raw
+
+        def w_copy(kind, a, c):
+            raw = st[("W", kind, a, c)]
+            grp = buf_bf16()
+            st[("grpW", kind, a, c)] = grp
+            if kind == "WM":
+                eng = wm_engine(a, c)
+                copy_on(
+                    eng,
+                    grp[:].rearrange("p (t m j) -> p t m j", t=4, j=4),
+                    raw[:].rearrange("p (j m t) -> p t m j", j=4, t=4),
+                )
+            else:
+                eng = GPS
+                copy_on(
+                    eng,
+                    grp[:].rearrange("p (n j) -> p n j", j=4),
+                    raw[:].rearrange("p (j n) -> p n j", j=4),
+                )
+            drop()
+            later(D_WQ if eng == GPS else 1, ("WQ", kind, a, c))
+
+        def w_quant(kind, a, c):
+            grp = st[("grpW", kind, a, c)]
+            codes = wm_codes if kind == "WM" else w1_codes
+            planes = wm_planes if kind == "WM" else w1_planes
+            nc.vector.quantize_mx(
+                out=codes[:, c, 512 * a : 512 * (a + 1)].bitcast(FP8X4),
+                scales=planes[4 * c : P, 512 * a : 512 * (a + 1)],
+                in_=grp[:],
+            )
+            drop()
+
+        def ta_bank(b, i, h):
+            words = st[("A", b, i)][:].bitcast(F32)
+            j, q = divmod(i, 4)
+            if h == 0:
+                st[("grpA", b, i)] = buf_bf16()
+                if q == 0:
+                    ac_new = work.tile([P, 4, 512], U32, name="ac", tag="ac", bufs=3, align_bytes=64)
+                    ap_new = work.tile([P, 512], U8, name="apl", tag="apl", bufs=3, align_bytes=64)
+                    st[("ac", b, j)] = ac_new
+                    st[("ap", b, j)] = ap_new
+            grp = st[("grpA", b, i)]
+            bank = psum.tile([P, 512], F32, name="tr", tag="tr", bufs=4)
+            for s in range(4):
+                c = 2 * h + s // 2
+                u = s % 2
+                nc.tensor.transpose(bank[:, P * s : P * (s + 1)], words[:, 256 * c + u : 256 * (c + 1) : 2], ident[:])
+            copy_on(
+                ta_engine(b, i, h),
+                grp[:].bitcast(F32)[:, 512 * h : 512 * (h + 1)].rearrange("p (c r u) -> p c r u", c=2, u=2),
+                bank[:].rearrange("p (c u r) -> p c r u", c=2, u=2),
+            )
+            later(D_QA, ("QA", b, i, h))
+            if h == 1:
+                drop()
+
+        def ta_quant(b, i, h):
+            j, q = divmod(i, 4)
+            grp = st[("grpA", b, i)]
+            ac = st[("ac", b, j)]
+            apl = st[("ap", b, j)]
+            for c in (2 * h, 2 * h + 1):
+                nc.vector.quantize_mx(
+                    out=ac[:, c, P * q : P * (q + 1)].bitcast(FP8X4),
+                    scales=apl[4 * c : P, P * q : P * (q + 1)],
+                    in_=grp[:, 512 * c : 512 * (c + 1)],
+                )
+            if h == 1:
+                drop()
+
+        def tx_bank(b, g, j, u):
+            words = st[("X", b, g, j)][:].bitcast(F32)
+            if j == 0:
+                xt_new = work.tile([P, NTOK], F32, name="xT", tag="xT", bufs=XT_BUFS)
+                st[("xT", b, g, u)] = xt_new
+            xt = st[("xT", b, g, u)]
+            bank = psum.tile([P, 512], F32, name="tr", tag="tr", bufs=4)
+            for q in range(4):
+                nc.tensor.transpose(bank[:, P * q : P * (q + 1)], words[:, 256 * q + u : 256 * (q + 1) : 2], ident[:])
+            nc.scalar.copy(out=xt[:, 512 * j : 512 * (j + 1)], in_=bank[:])
+            if u == 1:
+                drop()
+
+        def tb_bank(b, g, i):
+            bank = psum.tile([P, 512], F32, name="tr", tag="tr", bufs=4)
+            for t in range(4):
+                nc.tensor.transpose(bank[:, P * t : P * (t + 1)], st[("x2T", b, g, t)][:, P * i : P * (i + 1)], ident[:])
+            half = i % 2
+            if half == 0:
+                st[("xo", b, g, i // 2)] = buf_f32()
+            xo = st[("xo", b, g, i // 2)]
+            copy_on(
+                tb_engine(b, i),
+                xo[:, 512 * half : 512 * (half + 1)].rearrange("p (m t) -> p m t", t=4),
+                bank[:].rearrange("p (t m) -> p m t", t=4),
+            )
+            if half == 1:
+                later(D_ST, ("ST", b, g, i // 2))
+
+        def tb_store(b, g, i2):
+            nc.scalar.dma_start(
+                out=out_0[b, 256 * i2 : 256 * (i2 + 1), 512 * g : 512 * (g + 1)].rearrange("(i p) c -> p i c", p=P),
+                in_=st[("xo", b, g, i2)][:].rearrange("p (i c) -> p i c", i=2),
+            )
+            drop()
+
+        def mean_of(b, g, t):
+            sums = st[("sums", b, g, t)]
+            tot = small.tile([P, 1], F32, name="tot", tag="tot")
+            nmean = small.tile([P, 1], F32, name="nmean", tag="nmean")
+            nc.gpsimd.tensor_scalar(
+                out=tot[:], in0=sums[:, 0:1], scalar1=sums[:, 1:2], scalar2=sums[:, 2:3], op0=ALU.add, op1=ALU.add
+            )
+            nc.gpsimd.tensor_scalar(
+                out=nmean[:], in0=tot[:], scalar1=-1.0 / NTOK, scalar2=0.0, op0=ALU.mult, op1=ALU.add
+            )
+            st[("nmean", b, g, t)] = nmean
+            later(D_SQ, ("SQ", b, g, t))
+
+        def squares(b, g, t):
+            k = 4 * g + t
+            x2t = st[("x2T", b, g, t)]
+            nmean = st[("nmean", b, g, t)]
+            if ("xnb", b, g) not in st:
+                xnb_new = work.tile([P, 4, NTOK], BF16, name="xnb", tag="xnb", bufs=1)
+                st[("xnb", b, g)] = xnb_new
+            xnb = st[("xnb", b, g)]
+            ssq = small.tile([P, 1], F32, name="ssq", tag="ssq")
+            var = small.tile([P, 1], F32, name="var", tag="var")
+            rstd = small.tile([P, 1], F32, name="rstd", tag="rstd")
+            sc = small.tile([P, 1], F32, name="sc", tag="sc")
+            sh = small.tile([P, 1], F32, name="sh", tag="sh")
+            nc.scalar.activation(
+                out=xnb[:, t, :], in_=x2t[:], func=ACT.Square, bias=nmean[:], scale=1.0, accum_out=ssq[:]
+            )
+            nc.gpsimd.tensor_scalar(
+                out=var[:], in0=ssq[:], scalar1=1.0 / NTOK, scalar2=EPS, op0=ALU.mult, op1=ALU.add
+            )
+            nc.gpsimd.tensor_tensor(out=rstd[:], in0=var[:], in1=neg_half[:], op=ALU.pow)
+            nc.gpsimd.tensor_tensor(out=sc[:], in0=rstd[:], in1=ga[:, k : k + 1], op=ALU.mult)
+            nc.gpsimd.tensor_scalar(
+                out=sh[:], in0=nmean[:], scalar1=sc[:], scalar2=be[:, k : k + 1], op0=ALU.mult, op1=ALU.add
+            )
+            st[("sc", b, g, t)] = sc
+            st[("sh", b, g, t)] = sh
+            later(D_NRM, ("NRM", b, g, t))
+
+        def normalise(b, g, t):
+            xnb = st[("xnb", b, g)]
+            if nrm_engine(b, t) == VEC:
+                nc.vector.tensor_scalar(
+                    out=xnb[:, t, :],
+                    in0=st[("x2T", b, g, t)][:],
+                    scalar1=st[("sc", b, g, t)][:],
+                    scalar2=st[("sh", b, g, t)][:],
+                    op0=ALU.mult,
+                    op1=ALU.add,
+                )
+            else:
+                nc.scalar.activation(
+                    out=xnb[:, t, :],
+                    in_=st[("x2T", b, g, t)][:],
+                    func=ACT.Identity,
+                    bias=st[("sh", b, g, t)][:],
+                    scale=st[("sc", b, g, t)][:],
+                )
+            if t == 3:
+                ilv_wait.append((b, g, 0))
+                ilv_wait.append((b, g, 1))
+                ilv_wait.append((b, g, 2))
+
+        def interleave(b, g, j):
+            xnb = st[("xnb", b, g)]
+            grp = buf_bf16()
+            nc.vector.tensor_copy(
+                out=grp[:].rearrange("p (r t) -> p r t", t=4),
+                in_=xnb[:, :, 512 * j : 512 * (j + 1)].rearrange("p t r -> p r t"),
+            )
+            st[("grpX", b, g, j)] = grp
+            free_xn[0] = free_xn[0] - 4
+            later(D_QX, ("QX", b, g, j))
+
+        def xn_quant(b, g, j):
+            grp = st[("grpX", b, g, j)]
+            for q in range(4):
+                xc = work.tile([P, P], U32, name="xc", tag="xc", bufs=XN_BUFS, align_bytes=64)
+                xp = work.tile([P, P], U8, name="xp", tag="xp", bufs=XN_BUFS, align_bytes=64)
+                nc.vector.quantize_mx(out=xc[:].bitcast(FP8X4), scales=xp[:], in_=grp[:, 512 * q : 512 * (q + 1)])
+                st[("xc", b, g, 4 * j + q)] = xc
+                st[("xp", b, g, 4 * j + q)] = xp
+            drop()
+
+        def s1_group(b, g, t, j):
+            if j == 0:
+                x2t_new = work.tile([P, NTOK], F32, name="x2T", tag="x2T", bufs=X2T_BUFS)
+                sums_new = small.tile([P, 3], F32, name="sums", tag="sums")
+                st[("x2T", b, g, t)] = x2t_new
+                st[("sums", b, g, t)] = sums_new
+            x2t = st[("x2T", b, g, t)]
+            sums = st[("sums", b, g, t)]
+            ac = st[("ac", b, j)]
+            apl = st[("ap", b, j)]
+            col = 512 * g + P * t
+            acc = psum.tile([P, 512], F32, name="acc", tag="acc", bufs=4)
+            for c in range(4):
+                nc.tensor.matmul_mx(
+                    out=acc[:],
+                    lhsT=wm_codes[:, c, col : col + P].bitcast(FP8X4),
+                    lhsT_scale=wm_planes[4 * c : P, col : col + P],
+                    rhs=ac[:, c, :].bitcast(FP8X4),
+                    rhs_scale=apl[4 * c : P, :],
+                    start=(c == 0),
+                    stop=(c == 3),
+                )
+            u, e = divmod(t, 2)
+            xv = st[("xT", b, g, u)][:].bitcast(BF16)[:, 1024 * j + e : 1024 * (j + 1) : 2]
+            nc.vector.scalar_tensor_tensor(
+                out=x2t[:, 512 * j : 512 * (j + 1)],
+                in0=acc[:],
+                scalar=bm[:, 4 * g + t : 4 * g + t + 1],
+                in1=xv,
+                op0=ALU.add,
+                op1=ALU.add,
+                accum_out=sums[:, j : j + 1],
+            )
+            if j == 2:
+                mean_of(b, g, t)
+
+        def s2_group(b, i, e):
+            acc = psum.tile([P, 512], F32, name="acc", tag="acc", bufs=4)
+            for g in range(4):
+                nc.tensor.matmul_mx(
+                    out=acc[:],
+                    lhsT=st[("xc", b, g, i)][:].bitcast(FP8X4),
+                    lhsT_scale=st[("xp", b, g, i)][:],
+                    rhs=w1_codes[:, g, 512 * e : 512 * (e + 1)].bitcast(FP8X4),
+                    rhs_scale=w1_planes[4 * g : P, 512 * e : 512 * (e + 1)],
+                    start=(g == 0),
+                    stop=(g == 3),
+                )
+            half = e % 2
+            if half == 0:
+                st[("fo", b, i, e // 2)] = buf_f32()
+            fo = st[("fo", b, i, e // 2)]
+            nc.vector.tensor_tensor(
+                out=fo[:, 512 * half : 512 * (half + 1)], in0=acc[:], in1=b1_rows[:, 512 * e : 512 * (e + 1)], op=ALU.add
+            )
+            if half == 1:
+                nc.sync.dma_start(out=out_1[b, P * i : P * (i + 1), 512 * (e - 1) : 512 * (e + 1)], in_=fo[:])
+                drop()
+            if e == 3:
+                free_xn[0] = free_xn[0] + 4
+
+        def unit(b, g):
+            return [("S1", b, g, t, j) for t in range(4) for j in range(3)]
+
+        def s2_tiles(b, lo, hi):
+            return [("S2", b, i, e) for i in range(lo, hi) for e in range(4)]
+
+        def ta(b, lo, hi):
+            return [("TA", b, i, h) for i in range(lo, hi) for h in range(2)]
+
+        def tx(b, g, u):
+            return [("TX", b, g, j, u) for j in range(3)]
+
+        def tb(b, g):
+            return [("TB", b, g, i) for i in range(12)]
+
+        phases = []
+        phases.append(([], ta(0, 0, 12) + tx(0, 0, 0) + tx(0, 0, 1), RUN))
+        for b in range(4):
+            for g in range(4):
+                ug = unit(b, g)
+                nxt0 = tx(b, g + 1, 0) if g < 3 else []
+                nxt1 = tx(b, g + 1, 1) if g < 3 else []
+                if b == 0:
+                    if g == 0:
+                        phases.append((ug[0:6], [], RUN))
+                    else:
+                        phases.append((ug[0:3], tb(0, g - 1), RUN))
+                        phases.append((ug[3:6], tx(b, g, 1), 3))
+                    phases.append((ug[6:12], nxt0, 3))
+                    if g == 3:
+                        phases.append(([], tb(0, 3) + ta(1, 0, 12) + tx(1, 0, 0) + tx(1, 0, 1), RUN))
+                else:
+                    phases.append((ug[0:6], [], 3))
+                    phases.append((ug[6:12], nxt0, 3))
+                    trs = tb(b, g) + nxt1
+                    if g == 3 and b < 3:
+                        trs = trs + ta(b + 1, 0, 12) + tx(b + 1, 0, 0) + tx(b + 1, 0, 1)
+                    phases.append((s2_tiles(b - 1, 3 * g, 3 * g + 3), trs, RUN))
+        phases.append((s2_tiles(3, 0, 12), [], RUN))
+
+        pe_seq = []
+        for ph in phases:
+            mx, trs, run = ph
+            n_mx = len(mx)
+            n_runs = (len(trs) + run - 1) // run
+            if n_mx == 0:
+                pe_seq.extend(trs)
+            else:
+                for n in range(n_mx):
+                    for r in range(n_runs):
+                        if (r * n_mx) // n_runs == n:
+                            pe_seq.extend(trs[run * r : run * (r + 1)])
+                    pe_seq.append(mx[n])
+
+        w_rest = [("WC", "WM", a, c) for a in range(1, 4) for c in range(4)]
+        w_rest = w_rest + [("WC", "W1", a, c) for a in range(4) for c in range(4)]
+        seq = [("WC", "WM", 0, c) for c in range(4)]
+        for n in range(len(pe_seq)):
+            if n >= W_START and (n - W_START) % W_EVERY == 0 and len(w_rest) > 0:
+                seq.append(w_rest.pop(0))
+            seq.append(pe_seq[n])
+
+        def load_key(item):
+            if item[0] == "TA":
+                return ("A", item[1], item[2])
+            if item[0] == "TX":
+                return ("X", item[1], item[2], item[3])
+            if item[0] == "WC":
+                return ("W", item[1], item[2], item[3])
+            return None
+
+        load_seq = []
+        seen = {}
+        for n in range(len(seq)):
+            key = load_key(seq[n])
+            if key is not None and key not in seen:
+                seen[key] = True
+                load_seq.append((n, key))
+        ptr = [0]
+
+        def emit(item):
+            kind = item[0]
+            if kind == "S1":
+                s1_group(item[1], item[2], item[3], item[4])
+            elif kind == "S2":
+                s2_group(item[1], item[2], item[3])
+            elif kind == "TA":
+                ta_bank(item[1], item[2], item[3])
+            elif kind == "TX":
+                tx_bank(item[1], item[2], item[3], item[4])
+            elif kind == "TB":
+                tb_bank(item[1], item[2], item[3])
+            elif kind == "WC":
+                w_copy(item[1], item[2], item[3])
+            elif kind == "WQ":
+                w_quant(item[1], item[2], item[3])
+            elif kind == "QA":
+                ta_quant(item[1], item[2], item[3])
+            elif kind == "ST":
+                tb_store(item[1], item[2], item[3])
+            elif kind == "SQ":
+                squares(item[1], item[2], item[3])
+            elif kind == "NRM":
+                normalise(item[1], item[2], item[3])
+            elif kind == "QX":
+                xn_quant(item[1], item[2], item[3])
+
+        nc.sync.dma_start(out=bm_bf[:], in_=b_merge.rearrange("(g p t) -> p g t", p=P, t=4))
+        nc.sync.dma_start(out=ga_bf[:], in_=gamma2.rearrange("a b (g p t) -> p (a b g) t", p=P, t=4))
+        nc.sync.dma_start(out=be_bf[:], in_=beta2.rearrange("a b (g p t) -> p (a b g) t", p=P, t=4))
+        nc.vector.tensor_copy(out=bm[:], in_=bm_bf[:].rearrange("p g t -> p (g t)"))
+        nc.vector.tensor_copy(out=ga[:], in_=ga_bf[:].rearrange("p g t -> p (g t)"))
+        nc.vector.tensor_copy(out=be[:], in_=be_bf[:].rearrange("p g t -> p (g t)"))
+
+        last_ilv = [-100]
+        n_seq = len(seq)
+        n = 0
+        while n < n_seq or len(todo) > 0 or len(ilv_wait) > 0:
+            now[0] = n
+            for item in todo.pop(n, []):
+                emit(item)
+            if len(ilv_wait) > 0 and free_xn[0] >= 4 and n - last_ilv[0] >= D_ILV:
+                nxt = ilv_wait.pop(0)
+                interleave(nxt[0], nxt[1], nxt[2])
+                last_ilv[0] = n
+            if n < n_seq:
+                if n == B1_AT:
+                    nc.sync.dma_start(out=b1_rows[:], in_=b1.partition_broadcast(P))
+                while ptr[0] < len(load_seq) and load_seq[ptr[0]][0] <= n + HORIZON and (
+                    live[0] < N_BUF - RESERVE or load_seq[ptr[0]][0] <= n
+                ):
+                    emit_load(load_seq[ptr[0]][1])
+                    ptr[0] = ptr[0] + 1
+                emit(seq[n])
+            n = n + 1

@@ -17,32 +17,36 @@ P = 128
 NTOK = 1536
 EPS = 1e-5
 
+VEC = 0
+SCA = 1
+GPS = 2
 N_BUF = 12
-RESERVE = 4
+RESERVE = 5
 XT_BUFS = 2
 X2T_BUFS = 5
 XN_BUFS = 48
 RUN = 4
+RUN_TB = 3
+RUN_T2 = 2
+PASSES = ((0, 1), (2, 3), (0, 1, 2, 3))
 HORIZON = 14
-D_SQ = 2
-D_NRM = 3
-D_ILV = 3
-D_QX = 1
-D_QA = 1
-D_ST = 1
-W_EVERY = 4
+D_SQ = 8
+D_NRM = 10
+D_ILV = 5
+D_QX = 3
+D_QA = 3
+D_ST = 4
+W_EVERY = 6
 W_START = 30
-D_WQ = 5
+D_WQ = (1, 3, 5)
+W_ENG = (VEC, SCA, VEC, SCA)
 B1_AT = 150
-VEC = 0
-SCA = 1
-GPS = 2
 
 
 def wm_engine(a, c):
     if a == 0:
         return (VEC, SCA, GPS, VEC)[c]
-    return GPS
+    return W_ENG[c]
 
 
 def nrm_engine(b, t):
@@ -160,14 +164,14 @@ def tile_attentionblock_pc_l_kernel(
                     raw[:].rearrange("p (j m t) -> p t m j", j=4, t=4),
                 )
             else:
-                eng = GPS
+                eng = W_ENG[c]
                 copy_on(
                     eng,
                     grp[:].rearrange("p (n j) -> p n j", j=4),
                     raw[:].rearrange("p (j n) -> p n j", j=4),
                 )
             drop()
-            later(D_WQ if eng == GPS else 1, ("WQ", kind, a, c))
+            later(D_WQ[eng], ("WQ", kind, a, c))
 
         def w_quant(kind, a, c):
             grp = st[("grpW", kind, a, c)]
@@ -341,8 +345,8 @@ def tile_attentionblock_pc_l_kernel(
                 st[("xp", b, g, 4 * j + q)] = xp
             drop()
 
-        def s1_group(b, g, t, j):
-            if j == 0:
+        def s1_group(b, g, t, j, part):
+            if j == 0 and part != 1:
                 x2t_new = work.tile([P, NTOK], F32, name="x2T", tag="x2T", bufs=X2T_BUFS)
                 sums_new = small.tile([P, 3], F32, name="sums", tag="sums")
                 st[("x2T", b, g, t)] = x2t_new
@@ -352,8 +356,11 @@ def tile_attentionblock_pc_l_kernel(
             ac = st[("ac", b, j)]
             apl = st[("ap", b, j)]
             col = 512 * g + P * t
-            acc = psum.tile([P, 512], F32, name="acc", tag="acc", bufs=4)
-            for c in range(4):
+            if part != 1:
+                acc_new = psum.tile([P, 512], F32, name="acc", tag="acc", bufs=4)
+                st["acc"] = acc_new
+            acc = st["acc"]
+            for c in PASSES[part]:
                 nc.tensor.matmul_mx(
                     out=acc[:],
                     lhsT=wm_codes[:, c, col : col + P].bitcast(FP8X4),
@@ -363,6 +370,8 @@ def tile_attentionblock_pc_l_kernel(
                     start=(c == 0),
                     stop=(c == 3),
                 )
+            if part == 0:
+                return
             u, e = divmod(t, 2)
             xv = st[("xT", b, g, u)][:].bitcast(BF16)[:, 1024 * j + e : 1024 * (j + 1) : 2]
             nc.vector.scalar_tensor_tensor(
@@ -377,9 +386,12 @@ def tile_attentionblock_pc_l_kernel(
             if j == 2:
                 mean_of(b, g, t)
 
-        def s2_group(b, i, e):
-            acc = psum.tile([P, 512], F32, name="acc", tag="acc", bufs=4)
-            for g in range(4):
+        def s2_group(b, i, e, part):
+            if part != 1:
+                acc_new = psum.tile([P, 512], F32, name="acc", tag="acc", bufs=4)
+                st["acc"] = acc_new
+            acc = st["acc"]
+            for g in PASSES[part]:
                 nc.tensor.matmul_mx(
                     out=acc[:],
                     lhsT=st[("xc", b, g, i)][:].bitcast(FP8X4),
@@ -389,6 +401,8 @@ def tile_attentionblock_pc_l_kernel(
                     start=(g == 0),
                     stop=(g == 3),
                 )
+            if part == 0:
+                return
             half = e % 2
             if half == 0:
                 st[("fo", b, i, e // 2)] = buf_f32()
@@ -403,13 +417,15 @@ def tile_attentionblock_pc_l_kernel(
                 free_xn[0] = free_xn[0] + 4
 
         def unit(b, g):
+            if g == 0:
+                return [("S1", b, g, t, j) for j in range(3) for t in range(4)]
             return [("S1", b, g, t, j) for t in range(4) for j in range(3)]
 
         def s2_tiles(b, lo, hi):
             return [("S2", b, i, e) for i in range(lo, hi) for e in range(4)]
 
-        def ta(b, lo, hi):
-            return [("TA", b, i, h) for i in range(lo, hi) for h in range(2)]
+        def chunk_in(b, j):
+            return [("TA", b, i, h) for i in range(4 * j, 4 * j + 4) for h in range(2)] + [("TX", b, 0, j, u) for u in range(2)]
 
         def tx(b, g, u):
             return [("TX", b, g, j, u) for j in range(3)]
@@ -418,43 +434,57 @@ def tile_attentionblock_pc_l_kernel(
             return [("TB", b, g, i) for i in range(12)]
 
         phases = []
-        phases.append(([], ta(0, 0, 12) + tx(0, 0, 0) + tx(0, 0, 1), RUN))
         for b in range(4):
+            old = s2_tiles(b - 2, 9, 12) if b >= 2 else []
+            phases.append((old, (tb(b - 1, 3) if b >= 1 else []) + chunk_in(b, 0)))
             for g in range(4):
                 ug = unit(b, g)
-                nxt0 = tx(b, g + 1, 0) if g < 3 else []
-                nxt1 = tx(b, g + 1, 1) if g < 3 else []
-                if b == 0:
-                    if g == 0:
-                        phases.append((ug[0:6], [], RUN))
-                    else:
-                        phases.append((ug[0:3], tb(0, g - 1), RUN))
-                        phases.append((ug[3:6], tx(b, g, 1), 3))
-                    phases.append((ug[6:12], nxt0, 3))
-                    if g == 3:
-                        phases.append(([], tb(0, 3) + ta(1, 0, 12) + tx(1, 0, 0) + tx(1, 0, 1), RUN))
+                if g == 0:
+                    phases.append((ug[0:4], chunk_in(b, 1)))
+                    phases.append((ug[4:8], chunk_in(b, 2)))
+                    phases.append((ug[8:12], []))
+                    if b == 0:
+                        phases.append(([], tx(b, 1, 0)))
+                elif b == 0:
+                    phases.append((ug[0:3], tb(0, g - 1)))
+                    phases.append((ug[3:6], tx(b, g, 1)))
+                    phases.append((ug[6:12], tx(b, g + 1, 0) if g < 3 else []))
                 else:
-                    phases.append((ug[0:6], [], 3))
-                    phases.append((ug[6:12], nxt0, 3))
-                    trs = tb(b, g) + nxt1
-                    if g == 3 and b < 3:
-                        trs = trs + ta(b + 1, 0, 12) + tx(b + 1, 0, 0) + tx(b + 1, 0, 1)
-                    phases.append((s2_tiles(b - 1, 3 * g, 3 * g + 3), trs, RUN))
-        phases.append((s2_tiles(3, 0, 12), [], RUN))
+                    phases.append((ug[0:6], []))
+                    phases.append((ug[6:12], tx(b, g + 1, 0) if g < 3 else []))
+                if b >= 1 and g < 3:
+                    trs = tb(b, g) + (tx(b, 1, 0) if g == 0 else []) + tx(b, g + 1, 1)
+                    phases.append((s2_tiles(b - 1, 3 * g, 3 * g + 3), trs))
+        phases.append((s2_tiles(2, 9, 12), tb(3, 3)))
+        phases.append((s2_tiles(3, 0, 12), []))
 
         pe_seq = []
         for ph in phases:
-            mx, trs, run = ph
-            n_mx = len(mx)
-            n_runs = (len(trs) + run - 1) // run
-            if n_mx == 0:
+            mx, trs = ph[0], ph[1]
+            runs = []
+            for item in trs:
+                cap = RUN_TB if item[0] == "TB" else RUN_T2
+                if len(runs) > 0 and runs[-1][0][0] == item[0] and len(runs[-1]) < cap:
+                    runs[-1].append(item)
+                else:
+                    runs.append([item])
+            if len(runs) > len(mx):
+                quanta = []
+                for item in mx:
+                    quanta.append(item + (0,))
+                    quanta.append(item + (1,))
+            else:
+                quanta = [item + (2,) for item in mx]
+            n_q = len(quanta)
+            n_r = len(runs)
+            if n_q == 0:
                 pe_seq.extend(trs)
             else:
-                for n in range(n_mx):
-                    for r in range(n_runs):
-                        if (r * n_mx) // n_runs == n:
-                            pe_seq.extend(trs[run * r : run * (r + 1)])
-                    pe_seq.append(mx[n])
+                for n in range(n_q):
+                    for r in range(n_r):
+                        if (r * n_q) // n_r == n:
+                            pe_seq.extend(runs[r])
+                    pe_seq.append(quanta[n])
 
         w_rest = [("WC", "WM", a, c) for a in range(1, 4) for c in range(4)]
         w_rest = w_rest + [("WC", "W1", a, c) for a in range(4) for c in range(4)]
@@ -485,9 +515,9 @@ def tile_attentionblock_pc_l_kernel(
         def emit(item):
             kind = item[0]
             if kind == "S1":
-                s1_group(item[1], item[2], item[3], item[4])
+                s1_group(item[1], item[2], item[3], item[4], item[5])
             elif kind == "S2":
-                s2_group(item[1], item[2], item[3])
+                s2_group(item[1], item[2], item[3], item[4])
             elif kind == "TA":
                 ta_bank(item[1], item[2], item[3])
             elif kind == "TX":

@@ -21,7 +21,7 @@ VEC = 0
 SCA = 1
 GPS = 2
 N_BUF = 12
-RESERVE = 5
+RESERVE = 4
 XT_BUFS = 2
 X2T_BUFS = 5
 XN_BUFS = 48
@@ -30,17 +30,26 @@ RUN_TB = 3
 RUN_T2 = 2
 PASSES = ((0, 1), (2, 3), (0, 1, 2, 3))
 HORIZON = 14
-D_SQ = 8
+D_SQ = 6
 D_NRM = 10
 D_ILV = 5
 D_QX = 3
-D_QA = 3
-D_ST = 4
-W_EVERY = 6
+D_QA = 2
+D_ST = 3
+W_EVERY = 4
 W_START = 30
 D_WQ = (1, 3, 5)
 W_ENG = (VEC, SCA, VEC, SCA)
 B1_AT = 150
+NRM0 = (VEC, VEC, VEC, VEC)
+NRM1 = (VEC, VEC, VEC, VEC)
+TB0 = (SCA,)
+TB1 = (SCA, SCA, SCA, VEC)
+TA0 = (VEC, SCA, SCA)
+TA1 = (SCA,)
+SORT_X = (None, SCA, SCA, SCA)
+SORT_A = (None, SCA)
+SORT_AHEAD = (4, 5, 8)
 
 
 def wm_engine(a, c):
@@ -51,20 +60,20 @@ def wm_engine(a, c):
 
 def nrm_engine(b, t):
     if b == 0:
-        return (SCA, VEC, SCA, VEC)[t]
-    return VEC
+        return NRM0[t]
+    return NRM1[t]
 
 
 def tb_engine(b, i):
     if b == 0:
-        return (SCA, SCA, VEC)[i % 3]
-    return SCA
+        return TB0[i % len(TB0)]
+    return TB1[i % len(TB1)]
 
 
 def ta_engine(b, i, h):
     if b == 0:
-        return (VEC, SCA)[h]
-    return SCA
+        return TA0[(2 * i + h) % len(TA0)]
+    return TA1[(2 * i + h) % len(TA1)]
 
 
 def tile_attentionblock_pc_l_kernel(
@@ -102,6 +111,7 @@ def tile_attentionblock_pc_l_kernel(
         live = [0]
         free_xn = [XN_BUFS]
         ilv_wait = []
+        held = []
 
         def later(d, item):
             when = now[0] + d
@@ -152,6 +162,36 @@ def tile_attentionblock_pc_l_kernel(
                 )
             st[key] = raw
 
+        def sort_engine(key):
+            if key[0] == "A":
+                return SORT_A[key[2] % len(SORT_A)]
+            return SORT_X[key[1]]
+
+        def sort_words(key):
+            raw = st[key]
+            srt = buf_bf16()
+            eng = sort_engine(key)
+            if eng == GPS:
+                copy_on(
+                    eng,
+                    srt[:].rearrange("p (u q e) -> p u q e", u=2, e=2),
+                    raw[:].rearrange("p (q u e) -> p u q e", u=2, e=2),
+                )
+            else:
+                copy_on(
+                    eng,
+                    srt[:].bitcast(F32).rearrange("p (u q) -> p u q", u=2),
+                    raw[:].bitcast(F32).rearrange("p (q u) -> p u q", u=2),
+                )
+            st[key] = srt
+            drop()
+
+        def words_of(key, blk, u):
+            words = st[key][:].bitcast(F32)
+            if sort_engine(key) is None:
+                return words[:, 256 * blk + u : 256 * (blk + 1) : 2]
+            return words[:, 512 * u + P * blk : 512 * u + P * (blk + 1)]
+
         def w_copy(kind, a, c):
             raw = st[("W", kind, a, c)]
             grp = buf_bf16()
@@ -185,32 +225,34 @@ def tile_attentionblock_pc_l_kernel(
             drop()
 
         def ta_bank(b, i, h):
-            words = st[("A", b, i)][:].bitcast(F32)
             j, q = divmod(i, 4)
             if h == 0:
                 st[("grpA", b, i)] = buf_bf16()
-                if q == 0:
-                    ac_new = work.tile([P, 4, 512], U32, name="ac", tag="ac", bufs=3, align_bytes=64)
-                    ap_new = work.tile([P, 512], U8, name="apl", tag="apl", bufs=3, align_bytes=64)
-                    st[("ac", b, j)] = ac_new
-                    st[("ap", b, j)] = ap_new
             grp = st[("grpA", b, i)]
-            bank = psum.tile([P, 512], F32, name="tr", tag="tr", bufs=4)
+            bank = psum.tile([P, 512], F32, name="tr", tag="ps", bufs=8)
             for s in range(4):
                 c = 2 * h + s // 2
                 u = s % 2
-                nc.tensor.transpose(bank[:, P * s : P * (s + 1)], words[:, 256 * c + u : 256 * (c + 1) : 2], ident[:])
+                nc.tensor.transpose(bank[:, P * s : P * (s + 1)], words_of(("A", b, i), c, u), ident[:])
             copy_on(
                 ta_engine(b, i, h),
                 grp[:].bitcast(F32)[:, 512 * h : 512 * (h + 1)].rearrange("p (c r u) -> p c r u", c=2, u=2),
                 bank[:].rearrange("p (c u r) -> p c r u", c=2, u=2),
             )
-            later(D_QA, ("QA", b, i, h))
+            if j == 0 and b >= 1 and ("freed", b - 1) not in st:
+                held.append(("QA", b, i, h))
+            else:
+                later(D_QA, ("QA", b, i, h))
             if h == 1:
                 drop()
 
         def ta_quant(b, i, h):
             j, q = divmod(i, 4)
+            if ("ac", b, j) not in st:
+                ac_new = work.tile([P, 4, 512], U32, name="ac", tag="ac", bufs=3, align_bytes=64)
+                ap_new = work.tile([P, 512], U8, name="apl", tag="apl", bufs=3, align_bytes=64)
+                st[("ac", b, j)] = ac_new
+                st[("ap", b, j)] = ap_new
             grp = st[("grpA", b, i)]
             ac = st[("ac", b, j)]
             apl = st[("ap", b, j)]
@@ -224,20 +266,19 @@ def tile_attentionblock_pc_l_kernel(
                 drop()
 
         def tx_bank(b, g, j, u):
-            words = st[("X", b, g, j)][:].bitcast(F32)
             if j == 0:
                 xt_new = work.tile([P, NTOK], F32, name="xT", tag="xT", bufs=XT_BUFS)
                 st[("xT", b, g, u)] = xt_new
             xt = st[("xT", b, g, u)]
-            bank = psum.tile([P, 512], F32, name="tr", tag="tr", bufs=4)
+            bank = psum.tile([P, 512], F32, name="tr", tag="ps", bufs=8)
             for q in range(4):
-                nc.tensor.transpose(bank[:, P * q : P * (q + 1)], words[:, 256 * q + u : 256 * (q + 1) : 2], ident[:])
+                nc.tensor.transpose(bank[:, P * q : P * (q + 1)], words_of(("X", b, g, j), q, u), ident[:])
             nc.scalar.copy(out=xt[:, 512 * j : 512 * (j + 1)], in_=bank[:])
             if u == 1:
                 drop()
 
         def tb_bank(b, g, i):
-            bank = psum.tile([P, 512], F32, name="tr", tag="tr", bufs=4)
+            bank = psum.tile([P, 512], F32, name="tr", tag="ps", bufs=8)
             for t in range(4):
                 nc.tensor.transpose(bank[:, P * t : P * (t + 1)], st[("x2T", b, g, t)][:, P * i : P * (i + 1)], ident[:])
             half = i % 2
@@ -357,7 +398,7 @@ def tile_attentionblock_pc_l_kernel(
             apl = st[("ap", b, j)]
             col = 512 * g + P * t
             if part != 1:
-                acc_new = psum.tile([P, 512], F32, name="acc", tag="acc", bufs=4)
+                acc_new = psum.tile([P, 512], F32, name="acc", tag="ps", bufs=8)
                 st["acc"] = acc_new
             acc = st["acc"]
             for c in PASSES[part]:
@@ -372,6 +413,12 @@ def tile_attentionblock_pc_l_kernel(
                 )
             if part == 0:
                 return
+            if g == 3 and t == 3 and j == 0:
+                st[("freed", b)] = True
+                for k in range(len(held)):
+                    later(1 + k // 2, held[k])
+                for k in range(len(held)):
+                    held.pop()
             u, e = divmod(t, 2)
             xv = st[("xT", b, g, u)][:].bitcast(BF16)[:, 1024 * j + e : 1024 * (j + 1) : 2]
             nc.vector.scalar_tensor_tensor(
@@ -388,7 +435,7 @@ def tile_attentionblock_pc_l_kernel(
 
         def s2_group(b, i, e, part):
             if part != 1:
-                acc_new = psum.tile([P, 512], F32, name="acc", tag="acc", bufs=4)
+                acc_new = psum.tile([P, 512], F32, name="acc", tag="ps", bufs=8)
                 st["acc"] = acc_new
             acc = st["acc"]
             for g in PASSES[part]:
@@ -425,7 +472,13 @@ def tile_attentionblock_pc_l_kernel(
             return [("S2", b, i, e) for i in range(lo, hi) for e in range(4)]
 
         def chunk_in(b, j):
-            return [("TA", b, i, h) for i in range(4 * j, 4 * j + 4) for h in range(2)] + [("TX", b, 0, j, u) for u in range(2)]
+            return ta_in(b, j) + tx_in(b, j)
+
+        def ta_in(b, j):
+            return [("TA", b, i, h) for i in range(4 * j, 4 * j + 4) for h in range(2)]
+
+        def tx_in(b, j):
+            return [("TX", b, 0, j, u) for u in range(2)]
 
         def tx(b, g, u):
             return [("TX", b, g, j, u) for j in range(3)]
@@ -436,7 +489,7 @@ def tile_attentionblock_pc_l_kernel(
         phases = []
         for b in range(4):
             old = s2_tiles(b - 2, 9, 12) if b >= 2 else []
-            phases.append((old, (tb(b - 1, 3) if b >= 1 else []) + chunk_in(b, 0)))
+            phases.append((old, (tb(b - 1, 3) + tx_in(b, 0)) if b >= 1 else chunk_in(b, 0)))
             for g in range(4):
                 ug = unit(b, g)
                 if g == 0:
@@ -448,22 +501,31 @@ def tile_attentionblock_pc_l_kernel(
                 elif b == 0:
                     phases.append((ug[0:3], tb(0, g - 1)))
                     phases.append((ug[3:6], tx(b, g, 1)))
-                    phases.append((ug[6:12], tx(b, g + 1, 0) if g < 3 else []))
+                    phases.append((ug[6:12], tx(b, g + 1, 0) if g < 3 else ta_in(b + 1, 0)))
                 else:
                     phases.append((ug[0:6], []))
-                    phases.append((ug[6:12], tx(b, g + 1, 0) if g < 3 else []))
+                    phases.append((ug[6:12], tx(b, g + 1, 0) if g < 3 else (ta_in(b + 1, 0) if b < 3 else [])))
                 if b >= 1 and g < 3:
                     trs = tb(b, g) + (tx(b, 1, 0) if g == 0 else []) + tx(b, g + 1, 1)
                     phases.append((s2_tiles(b - 1, 3 * g, 3 * g + 3), trs))
         phases.append((s2_tiles(2, 9, 12), tb(3, 3)))
         phases.append((s2_tiles(3, 0, 12), []))
 
+        def data_key(item):
+            if item[0] == "TA":
+                return ("A", item[1], item[2])
+            if item[0] == "TX":
+                return ("X", item[1], item[2], item[3])
+            return None
+
         pe_seq = []
         for ph in phases:
             mx, trs = ph[0], ph[1]
             runs = []
             for item in trs:
-                cap = RUN_TB if item[0] == "TB" else RUN_T2
+                cap = RUN_T2
+                if item[0] == "TB" or sort_engine(data_key(item)) is not None:
+                    cap = RUN_TB
                 if len(runs) > 0 and runs[-1][0][0] == item[0] and len(runs[-1]) < cap:
                     runs[-1].append(item)
                 else:
@@ -494,11 +556,28 @@ def tile_attentionblock_pc_l_kernel(
                 seq.append(w_rest.pop(0))
             seq.append(pe_seq[n])
 
+        sort_at = {}
+        seen_s = {}
+        for n in range(len(seq)):
+            key = data_key(seq[n])
+            if key is not None and key not in seen_s:
+                seen_s[key] = True
+                if sort_engine(key) is not None:
+                    at = max(0, n - SORT_AHEAD[sort_engine(key)])
+                    if at not in sort_at:
+                        sort_at[at] = []
+                    sort_at[at].append(("SRT", key))
+        seq_old = seq
+        seq = []
+        for n in range(len(seq_old)):
+            seq.extend(sort_at.get(n, []))
+            seq.append(seq_old[n])
+
         def load_key(item):
-            if item[0] == "TA":
-                return ("A", item[1], item[2])
-            if item[0] == "TX":
-                return ("X", item[1], item[2], item[3])
+            if item[0] == "SRT":
+                return item[1]
+            if item[0] == "TA" or item[0] == "TX":
+                return data_key(item)
             if item[0] == "WC":
                 return ("W", item[1], item[2], item[3])
             return None
@@ -524,6 +603,8 @@ def tile_attentionblock_pc_l_kernel(
                 tx_bank(item[1], item[2], item[3], item[4])
             elif kind == "TB":
                 tb_bank(item[1], item[2], item[3])
+            elif kind == "SRT":
+                sort_words(item[1])
             elif kind == "WC":
                 w_copy(item[1], item[2], item[3])
             elif kind == "WQ":

@@ -28,6 +28,7 @@ XN_BUFS = 48
 RUN = 4
 RUN_TB = 3
 RUN_T2 = 2
+RUN_TX = 3
 PASSES = ((0, 1), (2, 3), (0, 1, 2, 3))
 HORIZON = 14
 D_SQ = 6
@@ -47,8 +48,8 @@ TB0 = (SCA,)
 TB1 = (SCA, SCA, SCA, VEC)
 TA0 = (VEC, SCA, SCA)
 TA1 = (SCA,)
-SORT_X = (None, SCA, SCA, SCA)
-SORT_A = (None, SCA)
+SORT_X = (None, None, None, None)
+SORT_A = (None,)
 SORT_AHEAD = (4, 5, 8)
 
 
@@ -207,8 +208,8 @@ def tile_attentionblock_pc_l_kernel(
                 eng = W_ENG[c]
                 copy_on(
                     eng,
-                    grp[:].rearrange("p (n j) -> p n j", j=4),
-                    raw[:].rearrange("p (j n) -> p n j", j=4),
+                    grp[:].rearrange("p (c i j) -> p c j i", i=4, j=4),
+                    raw[:].rearrange("p (j c i) -> p c j i", j=4, i=4),
                 )
             drop()
             later(D_WQ[eng], ("WQ", kind, a, c))
@@ -369,8 +370,8 @@ def tile_attentionblock_pc_l_kernel(
             xnb = st[("xnb", b, g)]
             grp = buf_bf16()
             nc.vector.tensor_copy(
-                out=grp[:].rearrange("p (r t) -> p r t", t=4),
-                in_=xnb[:, :, 512 * j : 512 * (j + 1)].rearrange("p t r -> p r t"),
+                out=grp[:].rearrange("p (c i t) -> p c t i", i=4, t=4),
+                in_=xnb[:, :, 512 * j : 512 * (j + 1)].rearrange("p t (c i) -> p c t i", i=4),
             )
             st[("grpX", b, g, j)] = grp
             free_xn[0] = free_xn[0] - 4
@@ -526,6 +527,8 @@ def tile_attentionblock_pc_l_kernel(
                 cap = RUN_T2
                 if item[0] == "TB" or sort_engine(data_key(item)) is not None:
                     cap = RUN_TB
+                elif item[0] == "TX" and item[2] > 0:
+                    cap = RUN_TX
                 if len(runs) > 0 and runs[-1][0][0] == item[0] and len(runs[-1]) < cap:
                     runs[-1].append(item)
                 else:

@@ -27,8 +27,9 @@ X2T_BUFS = 5
 XN_BUFS = 48
 RUN = 4
 RUN_TB = 3
-RUN_T2 = 2
+RUN_T2 = 4
 RUN_TX = 3
+SHIFT_TB = 2
 PASSES = ((0, 1), (2, 3), (0, 1, 2, 3))
 HORIZON = 14
 D_SQ = 6
@@ -36,16 +37,17 @@ D_NRM = 10
 D_ILV = 5
 D_QX = 3
 D_QA = 2
-D_ST = 3
+D_ST = 4
 W_EVERY = 4
 W_START = 30
 D_WQ = (1, 3, 5)
 W_ENG = (VEC, SCA, VEC, SCA)
 B1_AT = 150
+ILV_ENG = ((VEC, VEC, VEC), (VEC, VEC, VEC), (VEC, VEC, VEC), (VEC, VEC, VEC))
 NRM0 = (VEC, VEC, VEC, VEC)
 NRM1 = (VEC, VEC, VEC, VEC)
 TB0 = (SCA,)
-TB1 = (SCA, SCA, SCA, VEC)
+TB1 = (SCA, VEC)
 TA0 = (VEC, SCA, SCA)
 TA1 = (SCA,)
 SORT_X = (None, None, None, None)
@@ -369,9 +371,10 @@ def tile_attentionblock_pc_l_kernel(
         def interleave(b, g, j):
             xnb = st[("xnb", b, g)]
             grp = buf_bf16()
-            nc.vector.tensor_copy(
-                out=grp[:].rearrange("p (c i t) -> p c t i", i=4, t=4),
-                in_=xnb[:, :, 512 * j : 512 * (j + 1)].rearrange("p t (c i) -> p c t i", i=4),
+            copy_on(
+                ILV_ENG[b][j],
+                grp[:].rearrange("p (c i t) -> p c t i", i=4, t=4),
+                xnb[:, :, 512 * j : 512 * (j + 1)].rearrange("p t (c i) -> p c t i", i=4),
             )
             st[("grpX", b, g, j)] = grp
             free_xn[0] = free_xn[0] - 4
@@ -545,9 +548,10 @@ def tile_attentionblock_pc_l_kernel(
             if n_q == 0:
                 pe_seq.extend(trs)
             else:
+                shift = SHIFT_TB if runs and runs[0][0][0] == "TB" else 0
                 for n in range(n_q):
                     for r in range(n_r):
-                        if (r * n_q) // n_r == n:
+                        if min(n_q - 1, (r * n_q) // n_r + shift) == n:
                             pe_seq.extend(runs[r])
                     pe_seq.append(quanta[n])
 

from contextlib import ExitStack

import concourse.mybir as mybir
from concourse.masks import make_identity

FLOPS = 2 * 2 * 4 * 1536 * 2048 * 2048

F32 = mybir.dt.float32
BF16 = mybir.dt.bfloat16
U32 = mybir.dt.uint32
U8 = mybir.dt.uint8
FP8X4 = mybir.dt.float8_e4m3fn_x4
ALU = mybir.AluOpType
ACT = mybir.ActivationFunctionType

P = 128
NTOK = 1536
EPS = 1e-5

VEC = 0
SCA = 1
GPS = 2
N_BUF = 12
RESERVE = 4
XT_BUFS = 2
X2T_BUFS = 5
XN_BUFS = 48
RUN = 4
RUN_TB = 3
RUN_T2 = 4
RUN_TX = 3
SHIFT_TB = 2
PASSES = ((0, 1), (2, 3), (0, 1, 2, 3))
HORIZON = 14
D_SQ = 6
D_NRM = 10
D_ILV = 5
D_QX = 3
D_QA = 2
D_ST = 4
W_EVERY = 4
W_START = 30
D_WQ = (1, 3, 5)
W_ENG = (VEC, SCA, VEC, SCA)
B1_AT = 150
ILV_ENG = ((VEC, VEC, VEC), (VEC, VEC, VEC), (VEC, VEC, VEC), (VEC, VEC, VEC))
NRM0 = (VEC, VEC, VEC, VEC)
NRM1 = (VEC, VEC, VEC, VEC)
TB0 = (SCA,)
TB1 = (SCA, VEC)
TA0 = (VEC, SCA, SCA)
TA1 = (SCA,)
SORT_X = (None, None, None, None)
SORT_A = (None,)
SORT_AHEAD = (4, 5, 8)


def wm_engine(a, c):
    if a == 0:
        return (VEC, SCA, GPS, VEC)[c]
    return W_ENG[c]


def nrm_engine(b, t):
    if b == 0:
        return NRM0[t]
    return NRM1[t]


def tb_engine(b, i):
    if b == 0:
        return TB0[i % len(TB0)]
    return TB1[i % len(TB1)]


def ta_engine(b, i, h):
    if b == 0:
        return TA0[(2 * i + h) % len(TA0)]
    return TA1[(2 * i + h) % len(TA1)]


def tile_attentionblock_pc_l_kernel(
    tc, attn_out, x, W_merge, b_merge, gamma2, beta2, W1, b1, out_0, out_1
):
    nc = tc.nc
    with ExitStack() as ctx:
        keep = ctx.enter_context(tc.tile_pool(name="keep", bufs=1))
        work = ctx.enter_context(tc.tile_pool(name="work", bufs=2))
        small = ctx.enter_context(tc.tile_pool(name="small", bufs=8))
        psum = ctx.enter_context(tc.psum_pool(name="psum", bufs=4))
        ctx.enter_context(tc.manual_schedule())

        ident = keep.tile([P, P], F32, name="ident")
        make_identity(nc, ident[:])
        neg_half = keep.tile([P, 1], F32, name="neg_half")
        nc.vector.memset(neg_half[:], -0.5)

        wm_codes = keep.tile([P, 4, 2048], U32, name="wm_codes", align_bytes=64)
        wm_planes = keep.tile([P, 2048], U8, name="wm_planes", align_bytes=64)
        w1_codes = keep.tile([P, 4, 2048], U32, name="w1_codes", align_bytes=64)
        w1_planes = keep.tile([P, 2048], U8, name="w1_planes", align_bytes=64)
        b1_rows = keep.tile([P, 2048], BF16, name="b1_rows")

        bm_bf = keep.tile([P, 4, 4], BF16, name="bm_bf")
        ga_bf = keep.tile([P, 4, 4], BF16, name="ga_bf")
        be_bf = keep.tile([P, 4, 4], BF16, name="be_bf")
        bm = keep.tile([P, 16], F32, name="bm")
        ga = keep.tile([P, 16], F32, name="ga")
        be = keep.tile([P, 16], F32, name="be")

        st = {}
        todo = {}
        now = [0]
        live = [0]
        free_xn = [XN_BUFS]
        ilv_wait = []
        held = []

        def later(d, item):
            when = now[0] + d
            if when not in todo:
                todo[when] = []
            todo[when].append(item)

        def buf_bf16():
            live[0] = live[0] + 1
            assert live[0] <= N_BUF
            buf = work.tile([P, 2048], BF16, name="buf", tag="buf", bufs=N_BUF, align_bytes=64)
            return buf

        def buf_f32():
            live[0] = live[0] + 1
            assert live[0] <= N_BUF
            buf = work.tile([P, 1024], F32, name="buf", tag="buf", bufs=N_BUF, align_bytes=64)
            return buf

        def drop():
            live[0] = live[0] - 1

        def copy_on(which, out, in_):
            if which == VEC:
                nc.vector.tensor_copy(out=out, in_=in_)
            elif which == SCA:
                nc.scalar.copy(out=out, in_=in_)
            else:
                nc.gpsimd.tensor_scalar(out=out, in0=in_, scalar1=1.0, scalar2=0.0, op0=ALU.mult, op1=ALU.add)

        def emit_load(key):
            raw = buf_bf16()
            if key[0] == "W":
                src = W_merge if key[1] == "WM" else W1
                a, c = key[2], key[3]
                nc.sync.dma_start(
                    out=raw[:].rearrange("p (j n) -> p j n", j=4),
                    in_=src[512 * c : 512 * (c + 1), 512 * a : 512 * (a + 1)].rearrange("(p j) n -> p j n", j=4),
                )
            elif key[0] == "A":
                b, i = key[1], key[2]
                nc.sync.dma_start(out=raw[:], in_=attn_out[b, P * i : P * (i + 1), :])
            else:
                b, g, j = key[1], key[2], key[3]
                nc.sync.dma_start(
                    out=raw[:].rearrange("p (i c) -> p i c", i=4),
                    in_=x[b, 512 * j : 512 * (j + 1), 512 * g : 512 * (g + 1)].rearrange("(i p) c -> p i c", p=P),
                )
            st[key] = raw

        def sort_engine(key):
            if key[0] == "A":
                return SORT_A[key[2] % len(SORT_A)]
            return SORT_X[key[1]]

        def sort_words(key):
            raw = st[key]
            srt = buf_bf16()
            eng = sort_engine(key)
            if eng == GPS:
                copy_on(
                    eng,
                    srt[:].rearrange("p (u q e) -> p u q e", u=2, e=2),
                    raw[:].rearrange("p (q u e) -> p u q e", u=2, e=2),
                )
            else:
                copy_on(
                    eng,
                    srt[:].bitcast(F32).rearrange("p (u q) -> p u q", u=2),
                    raw[:].bitcast(F32).rearrange("p (q u) -> p u q", u=2),
                )
            st[key] = srt
            drop()

        def words_of(key, blk, u):
            words = st[key][:].bitcast(F32)
            if sort_engine(key) is None:
                return words[:, 256 * blk + u : 256 * (blk + 1) : 2]
            return words[:, 512 * u + P * blk : 512 * u + P * (blk + 1)]

        def w_copy(kind, a, c):
            raw = st[("W", kind, a, c)]
            grp = buf_bf16()
            st[("grpW", kind, a, c)] = grp
            if kind == "WM":
                eng = wm_engine(a, c)
                copy_on(
                    eng,
                    grp[:].rearrange("p (t m j) -> p t m j", t=4, j=4),
                    raw[:].rearrange("p (j m t) -> p t m j", j=4, t=4),
                )
            else:
                eng = W_ENG[c]
                copy_on(
                    eng,
                    grp[:].rearrange("p (c i j) -> p c j i", i=4, j=4),
                    raw[:].rearrange("p (j c i) -> p c j i", j=4, i=4),
                )
            drop()
            later(D_WQ[eng], ("WQ", kind, a, c))

        def w_quant(kind, a, c):
            grp = st[("grpW", kind, a, c)]
            codes = wm_codes if kind == "WM" else w1_codes
            planes = wm_planes if kind == "WM" else w1_planes
            nc.vector.quantize_mx(
                out=codes[:, c, 512 * a : 512 * (a + 1)].bitcast(FP8X4),
                scales=planes[4 * c : P, 512 * a : 512 * (a + 1)],
                in_=grp[:],
            )
            drop()

        def ta_bank(b, i, h):
            j, q = divmod(i, 4)
            if h == 0:
                st[("grpA", b, i)] = buf_bf16()
            grp = st[("grpA", b, i)]
            bank = psum.tile([P, 512], F32, name="tr", tag="ps", bufs=8)
            for s in range(4):
                c = 2 * h + s // 2
                u = s % 2
                nc.tensor.transpose(bank[:, P * s : P * (s + 1)], words_of(("A", b, i), c, u), ident[:])
            copy_on(
                ta_engine(b, i, h),
                grp[:].bitcast(F32)[:, 512 * h : 512 * (h + 1)].rearrange("p (c r u) -> p c r u", c=2, u=2),
                bank[:].rearrange("p (c u r) -> p c r u", c=2, u=2),
            )
            if j == 0 and b >= 1 and ("freed", b - 1) not in st:
                held.append(("QA", b, i, h))
            else:
                later(D_QA, ("QA", b, i, h))
            if h == 1:
                drop()

        def ta_quant(b, i, h):
            j, q = divmod(i, 4)
            if ("ac", b, j) not in st:
                ac_new = work.tile([P, 4, 512], U32, name="ac", tag="ac", bufs=3, align_bytes=64)
                ap_new = work.tile([P, 512], U8, name="apl", tag="apl", bufs=3, align_bytes=64)
                st[("ac", b, j)] = ac_new
                st[("ap", b, j)] = ap_new
            grp = st[("grpA", b, i)]
            ac = st[("ac", b, j)]
            apl = st[("ap", b, j)]
            for c in (2 * h, 2 * h + 1):
                nc.vector.quantize_mx(
                    out=ac[:, c, P * q : P * (q + 1)].bitcast(FP8X4),
                    scales=apl[4 * c : P, P * q : P * (q + 1)],
                    in_=grp[:, 512 * c : 512 * (c + 1)],
                )
            if h == 1:
                drop()

        def tx_bank(b, g, j, u):
            if j == 0:
                xt_new = work.tile([P, NTOK], F32, name="xT", tag="xT", bufs=XT_BUFS)
                st[("xT", b, g, u)] = xt_new
            xt = st[("xT", b, g, u)]
            bank = psum.tile([P, 512], F32, name="tr", tag="ps", bufs=8)
            for q in range(4):
                nc.tensor.transpose(bank[:, P * q : P * (q + 1)], words_of(("X", b, g, j), q, u), ident[:])
            nc.scalar.copy(out=xt[:, 512 * j : 512 * (j + 1)], in_=bank[:])
            if u == 1:
                drop()

        def tb_bank(b, g, i):
            bank = psum.tile([P, 512], F32, name="tr", tag="ps", bufs=8)
            for t in range(4):
                nc.tensor.transpose(bank[:, P * t : P * (t + 1)], st[("x2T", b, g, t)][:, P * i : P * (i + 1)], ident[:])
            half = i % 2
            if half == 0:
                st[("xo", b, g, i // 2)] = buf_f32()
            xo = st[("xo", b, g, i // 2)]
            copy_on(
                tb_engine(b, i),
                xo[:, 512 * half : 512 * (half + 1)].rearrange("p (m t) -> p m t", t=4),
                bank[:].rearrange("p (t m) -> p m t", t=4),
            )
            if half == 1:
                later(D_ST, ("ST", b, g, i // 2))

        def tb_store(b, g, i2):
            nc.scalar.dma_start(
                out=out_0[b, 256 * i2 : 256 * (i2 + 1), 512 * g : 512 * (g + 1)].rearrange("(i p) c -> p i c", p=P),
                in_=st[("xo", b, g, i2)][:].rearrange("p (i c) -> p i c", i=2),
            )
            drop()

        def mean_of(b, g, t):
            sums = st[("sums", b, g, t)]
            tot = small.tile([P, 1], F32, name="tot", tag="tot")
            nmean = small.tile([P, 1], F32, name="nmean", tag="nmean")
            nc.gpsimd.tensor_scalar(
                out=tot[:], in0=sums[:, 0:1], scalar1=sums[:, 1:2], scalar2=sums[:, 2:3], op0=ALU.add, op1=ALU.add
            )
            nc.gpsimd.tensor_scalar(
                out=nmean[:], in0=tot[:], scalar1=-1.0 / NTOK, scalar2=0.0, op0=ALU.mult, op1=ALU.add
            )
            st[("nmean", b, g, t)] = nmean
            later(D_SQ, ("SQ", b, g, t))

        def squares(b, g, t):
            k = 4 * g + t
            x2t = st[("x2T", b, g, t)]
            nmean = st[("nmean", b, g, t)]
            if ("xnb", b, g) not in st:
                xnb_new = work.tile([P, 4, NTOK], BF16, name="xnb", tag="xnb", bufs=1)
                st[("xnb", b, g)] = xnb_new
            xnb = st[("xnb", b, g)]
            ssq = small.tile([P, 1], F32, name="ssq", tag="ssq")
            var = small.tile([P, 1], F32, name="var", tag="var")
            rstd = small.tile([P, 1], F32, name="rstd", tag="rstd")
            sc = small.tile([P, 1], F32, name="sc", tag="sc")
            sh = small.tile([P, 1], F32, name="sh", tag="sh")
            nc.scalar.activation(
                out=xnb[:, t, :], in_=x2t[:], func=ACT.Square, bias=nmean[:], scale=1.0, accum_out=ssq[:]
            )
            nc.gpsimd.tensor_scalar(
                out=var[:], in0=ssq[:], scalar1=1.0 / NTOK, scalar2=EPS, op0=ALU.mult, op1=ALU.add
            )
            nc.gpsimd.tensor_tensor(out=rstd[:], in0=var[:], in1=neg_half[:], op=ALU.pow)
            nc.gpsimd.tensor_tensor(out=sc[:], in0=rstd[:], in1=ga[:, k : k + 1], op=ALU.mult)
            nc.gpsimd.tensor_scalar(
                out=sh[:], in0=nmean[:], scalar1=sc[:], scalar2=be[:, k : k + 1], op0=ALU.mult, op1=ALU.add
            )
            st[("sc", b, g, t)] = sc
            st[("sh", b, g, t)] = sh
            later(D_NRM, ("NRM", b, g, t))

        def normalise(b, g, t):
            xnb = st[("xnb", b, g)]
            if nrm_engine(b, t) == VEC:
                nc.vector.tensor_scalar(
                    out=xnb[:, t, :],
                    in0=st[("x2T", b, g, t)][:],
                    scalar1=st[("sc", b, g, t)][:],
                    scalar2=st[("sh", b, g, t)][:],
                    op0=ALU.mult,
                    op1=ALU.add,
                )
            else:
                nc.scalar.activation(
                    out=xnb[:, t, :],
                    in_=st[("x2T", b, g, t)][:],
                    func=ACT.Identity,
                    bias=st[("sh", b, g, t)][:],
                    scale=st[("sc", b, g, t)][:],
                )
            if t == 3:
                ilv_wait.append((b, g, 0))
                ilv_wait.append((b, g, 1))
                ilv_wait.append((b, g, 2))

        def interleave(b, g, j):
            xnb = st[("xnb", b, g)]
            grp = buf_bf16()
            copy_on(
                ILV_ENG[b][j],
                grp[:].rearrange("p (c i t) -> p c t i", i=4, t=4),
                xnb[:, :, 512 * j : 512 * (j + 1)].rearrange("p t (c i) -> p c t i", i=4),
            )
            st[("grpX", b, g, j)] = grp
            free_xn[0] = free_xn[0] - 4
            later(D_QX, ("QX", b, g, j))

        def xn_quant(b, g, j):
            grp = st[("grpX", b, g, j)]
            for q in range(4):
                xc = work.tile([P, P], U32, name="xc", tag="xc", bufs=XN_BUFS, align_bytes=64)
                xp = work.tile([P, P], U8, name="xp", tag="xp", bufs=XN_BUFS, align_bytes=64)
                nc.vector.quantize_mx(out=xc[:].bitcast(FP8X4), scales=xp[:], in_=grp[:, 512 * q : 512 * (q + 1)])
                st[("xc", b, g, 4 * j + q)] = xc
                st[("xp", b, g, 4 * j + q)] = xp
            drop()

        def s1_group(b, g, t, j, part):
            if j == 0 and part != 1:
                x2t_new = work.tile([P, NTOK], F32, name="x2T", tag="x2T", bufs=X2T_BUFS)
                sums_new = small.tile([P, 3], F32, name="sums", tag="sums")
                st[("x2T", b, g, t)] = x2t_new
                st[("sums", b, g, t)] = sums_new
            x2t = st[("x2T", b, g, t)]
            sums = st[("sums", b, g, t)]
            ac = st[("ac", b, j)]
            apl = st[("ap", b, j)]
            col = 512 * g + P * t
            if part != 1:
                acc_new = psum.tile([P, 512], F32, name="acc", tag="ps", bufs=8)
                st["acc"] = acc_new
            acc = st["acc"]
            for c in PASSES[part]:
                nc.tensor.matmul_mx(
                    out=acc[:],
                    lhsT=wm_codes[:, c, col : col + P].bitcast(FP8X4),
                    lhsT_scale=wm_planes[4 * c : P, col : col + P],
                    rhs=ac[:, c, :].bitcast(FP8X4),
                    rhs_scale=apl[4 * c : P, :],
                    start=(c == 0),
                    stop=(c == 3),
                )
            if part == 0:
                return
            if g == 3 and t == 3 and j == 0:
                st[("freed", b)] = True
                for k in range(len(held)):
                    later(1 + k // 2, held[k])
                for k in range(len(held)):
                    held.pop()
            u, e = divmod(t, 2)
            xv = st[("xT", b, g, u)][:].bitcast(BF16)[:, 1024 * j + e : 1024 * (j + 1) : 2]
            nc.vector.scalar_tensor_tensor(
                out=x2t[:, 512 * j : 512 * (j + 1)],
                in0=acc[:],
                scalar=bm[:, 4 * g + t : 4 * g + t + 1],
                in1=xv,
                op0=ALU.add,
                op1=ALU.add,
                accum_out=sums[:, j : j + 1],
            )
            if j == 2:
                mean_of(b, g, t)

        def s2_group(b, i, e, part):
            if part != 1:
                acc_new = psum.tile([P, 512], F32, name="acc", tag="ps", bufs=8)
                st["acc"] = acc_new
            acc = st["acc"]
            for g in PASSES[part]:
                nc.tensor.matmul_mx(
                    out=acc[:],
                    lhsT=st[("xc", b, g, i)][:].bitcast(FP8X4),
                    lhsT_scale=st[("xp", b, g, i)][:],
                    rhs=w1_codes[:, g, 512 * e : 512 * (e + 1)].bitcast(FP8X4),
                    rhs_scale=w1_planes[4 * g : P, 512 * e : 512 * (e + 1)],
                    start=(g == 0),
                    stop=(g == 3),
                )
            if part == 0:
                return
            half = e % 2
            if half == 0:
                st[("fo", b, i, e // 2)] = buf_f32()
            fo = st[("fo", b, i, e // 2)]
            nc.vector.tensor_tensor(
                out=fo[:, 512 * half : 512 * (half + 1)], in0=acc[:], in1=b1_rows[:, 512 * e : 512 * (e + 1)], op=ALU.add
            )
            if half == 1:
                nc.sync.dma_start(out=out_1[b, P * i : P * (i + 1), 512 * (e - 1) : 512 * (e + 1)], in_=fo[:])
                drop()
            if e == 3:
                free_xn[0] = free_xn[0] + 4

        def unit(b, g):
            if g == 0:
                return [("S1", b, g, t, j) for j in range(3) for t in range(4)]
            return [("S1", b, g, t, j) for t in range(4) for j in range(3)]

        def s2_tiles(b, lo, hi):
            return [("S2", b, i, e) for i in range(lo, hi) for e in range(4)]

        def chunk_in(b, j):
            return ta_in(b, j) + tx_in(b, j)

        def ta_in(b, j):
            return [("TA", b, i, h) for i in range(4 * j, 4 * j + 4) for h in range(2)]

        def tx_in(b, j):
            return [("TX", b, 0, j, u) for u in range(2)]

        def tx(b, g, u):
            return [("TX", b, g, j, u) for j in range(3)]

        def tb(b, g):
            return [("TB", b, g, i) for i in range(12)]

        phases = []
        for b in range(4):
            old = s2_tiles(b - 2, 9, 12) if b >= 2 else []
            phases.append((old, (tb(b - 1, 3) + tx_in(b, 0)) if b >= 1 else chunk_in(b, 0)))
            for g in range(4):
                ug = unit(b, g)
                if g == 0:
                    phases.append((ug[0:4], chunk_in(b, 1)))
                    phases.append((ug[4:8], chunk_in(b, 2)))
                    phases.append((ug[8:12], []))
                    if b == 0:
                        phases.append(([], tx(b, 1, 0)))
                elif b == 0:
                    phases.append((ug[0:3], tb(0, g - 1)))
                    phases.append((ug[3:6], tx(b, g, 1)))
                    phases.append((ug[6:12], tx(b, g + 1, 0) if g < 3 else ta_in(b + 1, 0)))
                else:
                    phases.append((ug[0:6], []))
                    phases.append((ug[6:12], tx(b, g + 1, 0) if g < 3 else (ta_in(b + 1, 0) if b < 3 else [])))
                if b >= 1 and g < 3:
                    trs = tb(b, g) + (tx(b, 1, 0) if g == 0 else []) + tx(b, g + 1, 1)
                    phases.append((s2_tiles(b - 1, 3 * g, 3 * g + 3), trs))
        phases.append((s2_tiles(2, 9, 12), tb(3, 3)))
        phases.append((s2_tiles(3, 0, 12), []))

        def data_key(item):
            if item[0] == "TA":
                return ("A", item[1], item[2])
            if item[0] == "TX":
                return ("X", item[1], item[2], item[3])
            return None

        pe_seq = []
        for ph in phases:
            mx, trs = ph[0], ph[1]
            runs = []
            for item in trs:
                cap = RUN_T2
                if item[0] == "TB" or sort_engine(data_key(item)) is not None:
                    cap = RUN_TB
                elif item[0] == "TX" and item[2] > 0:
                    cap = RUN_TX
                if len(runs) > 0 and runs[-1][0][0] == item[0] and len(runs[-1]) < cap:
                    runs[-1].append(item)
                else:
                    runs.append([item])
            if len(runs) > len(mx):
                quanta = []
                for item in mx:
                    quanta.append(item + (0,))
                    quanta.append(item + (1,))
            else:
                quanta = [item + (2,) for item in mx]
            n_q = len(quanta)
            n_r = len(runs)
            if n_q == 0:
                pe_seq.extend(trs)
            else:
                shift = SHIFT_TB if runs and runs[0][0][0] == "TB" else 0
                for n in range(n_q):
                    for r in range(n_r):
                        if min(n_q - 1, (r * n_q) // n_r + shift) == n:
                            pe_seq.extend(runs[r])
                    pe_seq.append(quanta[n])

        w_rest = [("WC", "WM", a, c) for a in range(1, 4) for c in range(4)]
        w_rest = w_rest + [("WC", "W1", a, c) for a in range(4) for c in range(4)]
        seq = [("WC", "WM", 0, c) for c in range(4)]
        for n in range(len(pe_seq)):
            if n >= W_START and (n - W_START) % W_EVERY == 0 and len(w_rest) > 0:
                seq.append(w_rest.pop(0))
            seq.append(pe_seq[n])

        sort_at = {}
        seen_s = {}
        for n in range(len(seq)):
            key = data_key(seq[n])
            if key is not None and key not in seen_s:
                seen_s[key] = True
                if sort_engine(key) is not None:
                    at = max(0, n - SORT_AHEAD[sort_engine(key)])
                    if at not in sort_at:
                        sort_at[at] = []
                    sort_at[at].append(("SRT", key))
        seq_old = seq
        seq = []
        for n in range(len(seq_old)):
            seq.extend(sort_at.get(n, []))
            seq.append(seq_old[n])

        def load_key(item):
            if item[0] == "SRT":
                return item[1]
            if item[0] == "TA" or item[0] == "TX":
                return data_key(item)
            if item[0] == "WC":
                return ("W", item[1], item[2], item[3])
            return None

        load_seq = []
        seen = {}
        for n in range(len(seq)):
            key = load_key(seq[n])
            if key is not None and key not in seen:
                seen[key] = True
                load_seq.append((n, key))
        ptr = [0]

        def emit(item):
            kind = item[0]
            if kind == "S1":
                s1_group(item[1], item[2], item[3], item[4], item[5])
            elif kind == "S2":
                s2_group(item[1], item[2], item[3], item[4])
            elif kind == "TA":
                ta_bank(item[1], item[2], item[3])
            elif kind == "TX":
                tx_bank(item[1], item[2], item[3], item[4])
            elif kind == "TB":
                tb_bank(item[1], item[2], item[3])
            elif kind == "SRT":
                sort_words(item[1])
            elif kind == "WC":
                w_copy(item[1], item[2], item[3])
            elif kind == "WQ":
                w_quant(item[1], item[2], item[3])
            elif kind == "QA":
                ta_quant(item[1], item[2], item[3])
            elif kind == "ST":
                tb_store(item[1], item[2], item[3])
            elif kind == "SQ":
                squares(item[1], item[2], item[3])
            elif kind == "NRM":
                normalise(item[1], item[2], item[3])
            elif kind == "QX":
                xn_quant(item[1], item[2], item[3])

        nc.sync.dma_start(out=bm_bf[:], in_=b_merge.rearrange("(g p t) -> p g t", p=P, t=4))
        nc.sync.dma_start(out=ga_bf[:], in_=gamma2.rearrange("a b (g p t) -> p (a b g) t", p=P, t=4))
        nc.sync.dma_start(out=be_bf[:], in_=beta2.rearrange("a b (g p t) -> p (a b g) t", p=P, t=4))
        nc.vector.tensor_copy(out=bm[:], in_=bm_bf[:].rearrange("p g t -> p (g t)"))
        nc.vector.tensor_copy(out=ga[:], in_=ga_bf[:].rearrange("p g t -> p (g t)"))
        nc.vector.tensor_copy(out=be[:], in_=be_bf[:].rearrange("p g t -> p (g t)"))

        last_ilv = [-100]
        n_seq = len(seq)
        n = 0
        while n < n_seq or len(todo) > 0 or len(ilv_wait) > 0:
            now[0] = n
            for item in todo.pop(n, []):
                emit(item)
            if len(ilv_wait) > 0 and free_xn[0] >= 4 and n - last_ilv[0] >= D_ILV:
                nxt = ilv_wait.pop(0)
                interleave(nxt[0], nxt[1], nxt[2])
                last_ilv[0] = n
            if n < n_seq:
                if n == B1_AT:
                    nc.sync.dma_start(out=b1_rows[:], in_=b1.partition_broadcast(P))
                while ptr[0] < len(load_seq) and load_seq[ptr[0]][0] <= n + HORIZON and (
                    live[0] < N_BUF - RESERVE or load_seq[ptr[0]][0] <= n
                ):
                    emit_load(load_seq[ptr[0]][1])
                    ptr[0] = ptr[0] + 1
                emit(seq[n])
            n = n + 1
